import numpy as np
import ml_dtypes


def mxq(x, axis, fmt="e4m3"):
    dtype, down = {"e4m3": (ml_dtypes.float8_e4m3fn, 7), "e5m2": (ml_dtypes.float8_e5m2, 14)}[fmt]
    v = np.moveaxis(np.asarray(x, np.float32).astype(ml_dtypes.bfloat16).astype(np.float64), axis, -1)
    blocks = v.reshape(v.shape[:-1] + (-1, 32))
    amax = np.abs(blocks).max(-1, keepdims=True)
    byte = np.maximum(np.where(amax > 0, np.frexp(amax)[1] - 1 + 127, 0) - down, 1)
    scale = np.exp2(byte - 127.0)
    codes = (blocks / scale).astype(np.float32).astype(dtype).astype(np.float64)
    return np.moveaxis((codes * scale).reshape(v.shape), -1, axis)


WIDE = False


def mx_kscale(k):
    if not WIDE:
        return np.ones(k)
    levels = np.array([10, -10, 5, -5, 0])
    a = np.random.permutation(np.resize(levels, k // 512 * 4)).reshape(k // 512, 4)
    idx = np.arange(k)
    return np.exp2(a[idx // 512, idx % 128 // 32])


BF16 = ml_dtypes.bfloat16


def bf(x):
    return np.asarray(x, np.float32).astype(BF16)


def f64(x):
    return np.asarray(x).astype(np.float64)


E2M1 = np.array([0.0, 0.5, 1.0, 1.5, 2.0, 3.0, 4.0, 6.0, -0.0, -0.5, -1.0, -1.5, -2.0, -3.0, -4.0, -6.0])


def pack_weight(w, fmt):
    k, n = w.shape
    w = f64(bf(w)).reshape(k // 32, 32, n)
    amax = np.abs(w).max(1)
    if fmt == "e4m3":
        byte = np.frexp(amax)[1] - 1 + 127 - 7
    else:
        mant, ex = np.frexp(amax / 6.0)
        byte = np.where(mant > 0.5, ex, ex - 1) + 127
    byte = np.clip(np.where(amax > 0, byte, 1), 1, 254)
    scaled = (w * np.exp2(127.0 - byte)[:, None, :]).reshape(k, n).astype(np.float32)
    by_word = np.ascontiguousarray(scaled.reshape(k // 512, 128, 4, n).transpose(0, 1, 3, 2))
    if fmt == "e4m3":
        words = by_word.astype(ml_dtypes.float8_e4m3fn).view(np.uint8)
    else:
        c = by_word.astype(ml_dtypes.float4_e2m1fn).view(np.uint8) & 0xF
        words = c[..., 0::2] | (c[..., 1::2] << 4)
    return np.ascontiguousarray(words), np.ascontiguousarray(byte.astype(np.uint8).reshape(k // 512, 16, n))


def unpack_weight(words, scales, fmt):
    g, p, n, _ = words.shape
    if fmt == "e4m3":
        vals = np.ascontiguousarray(words).view(ml_dtypes.float8_e4m3fn).astype(np.float64)
    else:
        nib = np.empty((g, p, n, 4), np.uint8)
        nib[..., 0::2] = words & 0xF
        nib[..., 1::2] = words >> 4
        vals = E2M1[nib]
    vals = vals * np.repeat(np.exp2(scales.astype(np.float64) - 127.0), 8, axis=1)[..., None]
    return vals.transpose(0, 1, 3, 2).reshape(g * 512, n)


B, HC, WC, C, F = 1024, 2, 2, 1024, 256


def setup_inputs():
    s = mx_kscale(C)
    x_crop = np.stack([np.random.standard_normal((B, HC, WC, C)), np.random.standard_normal((B, HC, WC, C))], axis=1)
    W_r = np.random.standard_normal((HC, WC, C, F)) * 0.5 / np.sqrt(C) / s[:, None]
    W_i = np.random.standard_normal((HC, WC, C, F)) * 0.5 / np.sqrt(C) / s[:, None]
    W_r_words, W_r_scales = pack_weight(W_r.reshape(-1, F), "e4m3")
    W_i_words, W_i_scales = pack_weight(W_i.reshape(-1, F), "e4m3")
    return {"x_crop": bf(x_crop * s),
            "W_r_words": W_r_words,
            "W_r_scales": W_r_scales,
            "W_i_words": W_i_words,
            "W_i_scales": W_i_scales,
            "b_r": bf(np.random.standard_normal(F) * 0.3),
            "b_i": bf(np.random.standard_normal(F) * 0.3)}


def reference(x_crop, W_r_words, W_r_scales, W_i_words, W_i_scales, b_r, b_i):
    sp = f64(x_crop)
    xr = mxq(sp[:, 0].transpose(1, 2, 0, 3), 3, "e4m3")
    xi = mxq(sp[:, 1].transpose(1, 2, 0, 3), 3, "e4m3")
    wr = unpack_weight(W_r_words, W_r_scales, "e4m3").reshape(HC, WC, C, F)
    wi = unpack_weight(W_i_words, W_i_scales, "e4m3").reshape(HC, WC, C, F)
    rr = xr @ wr
    ii = xi @ wi
    ri = xr @ wi
    ir = xi @ wr
    r = rr - ii + f64(b_r)
    i = ri + ir + f64(b_i)
    y = np.stack([r.transpose(2, 0, 1, 3), i.transpose(2, 0, 1, 3)], axis=1)
    return np.maximum(y, 0.0)

@@ -1,0 +1,186 @@
+from contextlib import ExitStack
+
+import concourse.mybir as mybir
+from concourse.masks import make_identity
+
+F32 = mybir.dt.float32
+BF16 = mybir.dt.bfloat16
+I32 = mybir.dt.int32
+U32 = mybir.dt.uint32
+U8 = mybir.dt.uint8
+FP8X4 = mybir.dt.float8_e4m3fn_x4
+ADD = mybir.AluOpType.add
+SUBTRACT = mybir.AluOpType.subtract
+RELU = mybir.ActivationFunctionType.Relu
+
+P = 128
+PACK = 4
+BATCH, PARTS, PIXEL_ROWS, PIXEL_COLS, CHANNELS = 1024, 2, 2, 2, 1024
+FEATURES = 256
+REAL, IMAG = 0, 1
+PASSES = CHANNELS // (P * PACK)
+WEIGHT_GROUPS = PIXEL_ROWS * PIXEL_COLS * PASSES
+ROUNDS = (BATCH // P) * PIXEL_ROWS
+X_AHEAD = 4
+
+FLOPS = 2 * 4 * BATCH * PIXEL_ROWS * PIXEL_COLS * CHANNELS * FEATURES
+
+
+def tile_dot_pa_t_e_kernel(
+    tc, x_crop, W_r_words, W_r_scales, W_i_words, W_i_scales, b_r, b_i, out
+):
+    nc = tc.nc
+    with ExitStack() as ctx:
+        const = ctx.enter_context(tc.tile_pool(name="const", bufs=1))
+        x_pool = ctx.enter_context(tc.tile_pool(name="x", bufs=X_AHEAD))
+        mx_pool = ctx.enter_context(tc.tile_pool(name="mx", bufs=2))
+        out_pool = ctx.enter_context(tc.tile_pool(name="out", bufs=2))
+        turned_pool = ctx.enter_context(tc.psum_pool(name="turned", bufs=4))
+        sum_pool = ctx.enter_context(tc.psum_pool(name="sums", bufs=1))
+        ctx.enter_context(tc.manual_schedule())
+
+        def rows_of(r):
+            return slice((r // PIXEL_ROWS) * P, (r // PIXEL_ROWS + 1) * P)
+
+        identity = const.tile([P, P], F32)
+        make_identity(nc, identity[:])
+        w_words = const.tile([P, PARTS, WEIGHT_GROUPS, FEATURES], U32, align_bytes=64)
+        w_planes = const.tile([P, PARTS, WEIGHT_GROUPS, FEATURES], U8, align_bytes=64)
+        nc.vector.memset(w_planes[:].rearrange("p a g n -> p (a g n)").bitcast(I32), 0)
+        bias = const.tile([P, PARTS, FEATURES], BF16)
+        nc.scalar.dma_start(out=bias[:, REAL, :], in_=b_r.partition_broadcast(P))
+        nc.scalar.dma_start(out=bias[:, IMAG, :], in_=b_i.partition_broadcast(P))
+
+        x_tiles = {}
+        quantised = {}
+        sums = {}
+        before_relu = {}
+
+        def load_x(r):
+            x_sb = x_pool.tile([P, PARTS, PIXEL_COLS, CHANNELS], BF16)
+            nc.sync.dma_start(out=x_sb[:], in_=x_crop[rows_of(r), :, r % PIXEL_ROWS, :, :])
+            x_tiles[r] = x_sb
+
+        def load_weight_scales():
+            for part, scales in enumerate((W_r_scales, W_i_scales)):
+                by_row = scales.bitcast(I32).rearrange("g (q j) n -> j q g n", j=4)
+                for j in range(4):
+                    nc.sync.dma_start(
+                        out=w_planes[j:P:32, part, :, :].bitcast(I32), in_=by_row[j]
+                    )
+
+        def load_weight_words(pixel_row):
+            groups = slice(
+                pixel_row * PIXEL_COLS * PASSES, (pixel_row + 1) * PIXEL_COLS * PASSES
+            )
+            for part, words in enumerate((W_r_words, W_i_words)):
+                as_words = words.rearrange("g p n t -> g p (n t)").bitcast(I32)
+                nc.sync.dma_start(
+                    out=w_words[:, part, groups, :].bitcast(I32),
+                    in_=as_words[groups].rearrange("g p n -> p g n"),
+                )
+
+        def transpose(r):
+            x_words = (
+                x_tiles[r][:]
+                .rearrange("p a w c -> p (a w c)")
+                .bitcast(F32)
+                .rearrange("p (s q u) -> p s u q", q=P, u=2)
+            )
+            grouped = mx_pool.tile([P, PIXEL_COLS, PARTS, PASSES, P, PACK], BF16, align_bytes=64)
+            grouped_words = (
+                grouped[:]
+                .rearrange("p w a g b t -> p (w a g b t)")
+                .bitcast(F32)
+                .rearrange("p (w a g b u) -> p w a g b u", w=PIXEL_COLS, a=PARTS, g=PASSES, u=2)
+            )
+            for col in range(PIXEL_COLS):
+                for part in range(PARTS):
+                    turned = turned_pool.tile([P, PASSES, 2, P], F32)
+                    for g in range(PASSES):
+                        for u in range(2):
+                            s = (part * PIXEL_COLS + col) * PASSES + g
+                            nc.tensor.transpose(turned[:, g, u, :], x_words[:, s, u, :], identity[:])
+                    nc.scalar.copy(
+                        out=grouped_words[:, col, part],
+                        in_=turned[:].rearrange("p g u b -> p g b u"),
+                    )
+            return grouped
+
+        def quantise(r, grouped):
+            codes = mx_pool.tile([P, PIXEL_COLS, PARTS, PASSES, P], U32, align_bytes=64)
+            planes = mx_pool.tile([P, PIXEL_COLS, PARTS, PASSES, P], U8, align_bytes=64)
+            for col in range(PIXEL_COLS):
+                nc.vector.quantize_mx(
+                    out=codes[:, col].rearrange("p a g b -> p (a g b)").bitcast(FP8X4),
+                    scales=planes[:, col].rearrange("p a g b -> p (a g b)"),
+                    in_=grouped[:, col].rearrange("p a g b t -> p (a g b t)"),
+                )
+            quantised[r] = (codes, planes)
+
+        def multiply(r):
+            codes, planes = quantised[r]
+            rr = sum_pool.tile([P, PIXEL_COLS, FEATURES], F32)
+            ii = sum_pool.tile([P, PIXEL_COLS, FEATURES], F32)
+            im = sum_pool.tile([P, PIXEL_COLS, FEATURES], F32)
+
+            def group(acc, col, products):
+                pixel = (r % PIXEL_ROWS) * PIXEL_COLS + col
+                passes = [(x_part, w_part, g) for x_part, w_part in products for g in range(PASSES)]
+                for n, (x_part, w_part, g) in enumerate(passes):
+                    nc.tensor.matmul_mx(
+                        out=acc[:, col, :],
+                        lhsT=codes[:, col, x_part, g, :].bitcast(FP8X4),
+                        lhsT_scale=planes[:, col, x_part, g, :],
+                        rhs=w_words[:, w_part, pixel * PASSES + g, :].bitcast(FP8X4),
+                        rhs_scale=w_planes[:, w_part, pixel * PASSES + g, :],
+                        start=(n == 0),
+                        stop=(n == len(passes) - 1),
+                    )
+
+            for col in range(PIXEL_COLS):
+                group(rr, col, [(REAL, REAL)])
+                group(ii, col, [(IMAG, IMAG)])
+                group(im, col, [(REAL, IMAG), (IMAG, REAL)])
+            sums[r] = (rr, ii, im)
+
+        def add_up(r):
+            rr, ii, im = sums[r]
+            shape = [P, PIXEL_COLS, FEATURES]
+            rr_biased = out_pool.tile(shape, F32)
+            y = out_pool.tile([P, PARTS, PIXEL_COLS, FEATURES], F32)
+            nc.vector.tensor_tensor(
+                out=rr_biased[:], in0=rr[:], in1=bias[:, REAL : REAL + 1, :].to_broadcast(shape), op=ADD
+            )
+            nc.vector.tensor_tensor(
+                out=y[:, IMAG], in0=im[:], in1=bias[:, IMAG : IMAG + 1, :].to_broadcast(shape), op=ADD
+            )
+            nc.vector.tensor_tensor(out=y[:, REAL], in0=rr_biased[:], in1=ii[:], op=SUBTRACT)
+            before_relu[r] = y
+
+        def relu_and_store(r):
+            result = out_pool.tile([P, PARTS, PIXEL_COLS, FEATURES], F32)
+            nc.scalar.activation(out=result[:], in_=before_relu[r][:], func=RELU)
+            nc.sync.dma_start(out=out[rows_of(r), :, r % PIXEL_ROWS, :, :], in_=result[:])
+
+        load_x(0)
+        load_x(1)
+        load_weight_scales()
+        load_weight_words(0)
+        load_x(2)
+        load_weight_words(1)
+        load_x(3)
+
+        for step in range(ROUNDS + 2):
+            if step < ROUNDS:
+                grouped = transpose(step)
+            if step + X_AHEAD < ROUNDS:
+                load_x(step + X_AHEAD)
+            if step >= 2:
+                add_up(step - 2)
+            if step < ROUNDS:
+                quantise(step, grouped)
+            if 1 <= step <= ROUNDS:
+                multiply(step - 1)
+            if step >= 2:
+                relu_and_store(step - 2)

@@ -21,7 +21,8 @@ REAL, IMAG = 0, 1
 PASSES = CHANNELS // (P * PACK)
 WEIGHT_GROUPS = PIXEL_ROWS * PIXEL_COLS * PASSES
 ROUNDS = (BATCH // P) * PIXEL_ROWS
-X_AHEAD = 4
+X_BUFS = 4
+SORT_AHEAD = 1
 
 FLOPS = 2 * 4 * BATCH * PIXEL_ROWS * PIXEL_COLS * CHANNELS * FEATURES
 
@@ -32,11 +33,12 @@ def tile_dot_pa_t_e_kernel(
     nc = tc.nc
     with ExitStack() as ctx:
         const = ctx.enter_context(tc.tile_pool(name="const", bufs=1))
-        x_pool = ctx.enter_context(tc.tile_pool(name="x", bufs=X_AHEAD))
+        x_pool = ctx.enter_context(tc.tile_pool(name="x", bufs=X_BUFS))
+        sorted_pool = ctx.enter_context(tc.tile_pool(name="sorted", bufs=SORT_AHEAD + 1))
         mx_pool = ctx.enter_context(tc.tile_pool(name="mx", bufs=2))
         out_pool = ctx.enter_context(tc.tile_pool(name="out", bufs=2))
         turned_pool = ctx.enter_context(tc.psum_pool(name="turned", bufs=4))
-        sum_pool = ctx.enter_context(tc.psum_pool(name="sums", bufs=1))
+        sum_pool = ctx.enter_context(tc.psum_pool(name="sums", bufs=4))
         ctx.enter_context(tc.manual_schedule())
 
         def rows_of(r):
@@ -52,6 +54,7 @@ def tile_dot_pa_t_e_kernel(
         nc.scalar.dma_start(out=bias[:, IMAG, :], in_=b_i.partition_broadcast(P))
 
         x_tiles = {}
+        sorted_tiles = {}
         quantised = {}
         sums = {}
         before_relu = {}
@@ -80,13 +83,24 @@ def tile_dot_pa_t_e_kernel(
                     in_=as_words[groups].rearrange("g p n -> p g n"),
                 )
 
-        def transpose(r):
+        def sort_words(r):
             x_words = (
                 x_tiles[r][:]
                 .rearrange("p a w c -> p (a w c)")
                 .bitcast(F32)
-                .rearrange("p (s q u) -> p s u q", q=P, u=2)
+                .rearrange("p (a w g q u) -> p a w g u q", a=PARTS, w=PIXEL_COLS, g=PASSES, u=2)
             )
+            x_sorted = sorted_pool.tile([P, PARTS, PIXEL_COLS, PASSES, 2, P], F32)
+            for part in range(PARTS):
+                for col in range(PIXEL_COLS):
+                    if (part, col) == (PARTS - 1, PIXEL_COLS - 1):
+                        nc.scalar.copy(out=x_sorted[:, part, col], in_=x_words[:, part, col])
+                    else:
+                        nc.vector.tensor_copy(out=x_sorted[:, part, col], in_=x_words[:, part, col])
+            sorted_tiles[r] = x_sorted
+
+        def transpose(r):
+            x_sorted = sorted_tiles[r]
             grouped = mx_pool.tile([P, PIXEL_COLS, PARTS, PASSES, P, PACK], BF16, align_bytes=64)
             grouped_words = (
                 grouped[:]
@@ -99,8 +113,9 @@ def tile_dot_pa_t_e_kernel(
                     turned = turned_pool.tile([P, PASSES, 2, P], F32)
                     for g in range(PASSES):
                         for u in range(2):
-                            s = (part * PIXEL_COLS + col) * PASSES + g
-                            nc.tensor.transpose(turned[:, g, u, :], x_words[:, s, u, :], identity[:])
+                            nc.tensor.transpose(
+                                turned[:, g, u, :], x_sorted[:, part, col, g, u, :], identity[:]
+                            )
                     nc.scalar.copy(
                         out=grouped_words[:, col, part],
                         in_=turned[:].rearrange("p g u b -> p g b u"),
@@ -120,9 +135,9 @@ def tile_dot_pa_t_e_kernel(
 
         def multiply(r):
             codes, planes = quantised[r]
-            rr = sum_pool.tile([P, PIXEL_COLS, FEATURES], F32)
-            ii = sum_pool.tile([P, PIXEL_COLS, FEATURES], F32)
-            im = sum_pool.tile([P, PIXEL_COLS, FEATURES], F32)
+            rr = sum_pool.tile([P, PIXEL_COLS, FEATURES], F32, tag="sum")
+            im = sum_pool.tile([P, PIXEL_COLS, FEATURES], F32, tag="sum")
+            ii = sum_pool.tile([P, PIXEL_COLS, FEATURES], F32, tag="sum")
 
             def group(acc, col, products):
                 pixel = (r % PIXEL_ROWS) * PIXEL_COLS + col
@@ -140,8 +155,10 @@ def tile_dot_pa_t_e_kernel(
 
             for col in range(PIXEL_COLS):
                 group(rr, col, [(REAL, REAL)])
-                group(ii, col, [(IMAG, IMAG)])
+            for col in range(PIXEL_COLS):
                 group(im, col, [(REAL, IMAG), (IMAG, REAL)])
+            for col in range(PIXEL_COLS):
+                group(ii, col, [(IMAG, IMAG)])
             sums[r] = (rr, ii, im)
 
         def add_up(r):
@@ -171,13 +188,19 @@ def tile_dot_pa_t_e_kernel(
         load_weight_words(1)
         load_x(3)
 
+        for r in range(SORT_AHEAD):
+            sort_words(r)
+            load_x(r + X_BUFS)
+
         for step in range(ROUNDS + 2):
             if step < ROUNDS:
                 grouped = transpose(step)
-            if step + X_AHEAD < ROUNDS:
-                load_x(step + X_AHEAD)
             if step >= 2:
                 add_up(step - 2)
+            if step + SORT_AHEAD < ROUNDS:
+                sort_words(step + SORT_AHEAD)
+            if step + SORT_AHEAD + X_BUFS < ROUNDS:
+                load_x(step + SORT_AHEAD + X_BUFS)
             if step < ROUNDS:
                 quantise(step, grouped)
             if 1 <= step <= ROUNDS:

@@ -9,9 +9,7 @@ I32 = mybir.dt.int32
 U32 = mybir.dt.uint32
 U8 = mybir.dt.uint8
 FP8X4 = mybir.dt.float8_e4m3fn_x4
-ADD = mybir.AluOpType.add
-SUBTRACT = mybir.AluOpType.subtract
-RELU = mybir.ActivationFunctionType.Relu
+ALU = mybir.AluOpType
 
 P = 128
 PACK = 4
@@ -22,7 +20,7 @@ PASSES = CHANNELS // (P * PACK)
 WEIGHT_GROUPS = PIXEL_ROWS * PIXEL_COLS * PASSES
 ROUNDS = (BATCH // P) * PIXEL_ROWS
 X_BUFS = 4
-SORT_AHEAD = 1
+LARGEST_F32 = 3.4028234663852886e38
 
 FLOPS = 2 * 4 * BATCH * PIXEL_ROWS * PIXEL_COLS * CHANNELS * FEATURES
 
@@ -34,9 +32,8 @@ def tile_dot_pa_t_e_kernel(
     with ExitStack() as ctx:
         const = ctx.enter_context(tc.tile_pool(name="const", bufs=1))
         x_pool = ctx.enter_context(tc.tile_pool(name="x", bufs=X_BUFS))
-        sorted_pool = ctx.enter_context(tc.tile_pool(name="sorted", bufs=SORT_AHEAD + 1))
         mx_pool = ctx.enter_context(tc.tile_pool(name="mx", bufs=2))
-        out_pool = ctx.enter_context(tc.tile_pool(name="out", bufs=2))
+        out_pool = ctx.enter_context(tc.tile_pool(name="out", bufs=3))
         turned_pool = ctx.enter_context(tc.psum_pool(name="turned", bufs=4))
         sum_pool = ctx.enter_context(tc.psum_pool(name="sums", bufs=4))
         ctx.enter_context(tc.manual_schedule())
@@ -61,7 +58,10 @@ def tile_dot_pa_t_e_kernel(
 
         def load_x(r):
             x_sb = x_pool.tile([P, PARTS, PIXEL_COLS, CHANNELS], BF16)
-            nc.sync.dma_start(out=x_sb[:], in_=x_crop[rows_of(r), :, r % PIXEL_ROWS, :, :])
+            for part in range(PARTS):
+                nc.sync.dma_start(
+                    out=x_sb[:, part], in_=x_crop[rows_of(r), part, r % PIXEL_ROWS, :, :]
+                )
             x_tiles[r] = x_sb
 
         def load_weight_scales():
@@ -88,48 +88,44 @@ def tile_dot_pa_t_e_kernel(
                 x_tiles[r][:]
                 .rearrange("p a w c -> p (a w c)")
                 .bitcast(F32)
-                .rearrange("p (a w g q u) -> p a w g u q", a=PARTS, w=PIXEL_COLS, g=PASSES, u=2)
+                .rearrange("p (a s q u) -> p a s u q", a=PARTS, q=P, u=2)
             )
-            x_sorted = sorted_pool.tile([P, PARTS, PIXEL_COLS, PASSES, 2, P], F32)
-            for part in range(PARTS):
-                for col in range(PIXEL_COLS):
-                    if (part, col) == (PARTS - 1, PIXEL_COLS - 1):
-                        nc.scalar.copy(out=x_sorted[:, part, col], in_=x_words[:, part, col])
-                    else:
-                        nc.vector.tensor_copy(out=x_sorted[:, part, col], in_=x_words[:, part, col])
+            x_sorted = mx_pool.tile([P, PARTS, PIXEL_COLS * PASSES, 2, P], F32)
+            nc.vector.tensor_copy(out=x_sorted[:, REAL], in_=x_words[:, REAL])
+            nc.scalar.copy(out=x_sorted[:, IMAG], in_=x_words[:, IMAG])
             sorted_tiles[r] = x_sorted
 
         def transpose(r):
             x_sorted = sorted_tiles[r]
-            grouped = mx_pool.tile([P, PIXEL_COLS, PARTS, PASSES, P, PACK], BF16, align_bytes=64)
+            grouped = mx_pool.tile([P, PARTS, PIXEL_COLS, PASSES, P, PACK], BF16, align_bytes=64)
             grouped_words = (
                 grouped[:]
-                .rearrange("p w a g b t -> p (w a g b t)")
+                .rearrange("p a w g b t -> p (a w g b t)")
                 .bitcast(F32)
-                .rearrange("p (w a g b u) -> p w a g b u", w=PIXEL_COLS, a=PARTS, g=PASSES, u=2)
+                .rearrange("p (a w g b u) -> p a w g b u", a=PARTS, w=PIXEL_COLS, g=PASSES, u=2)
             )
-            for col in range(PIXEL_COLS):
-                for part in range(PARTS):
+            for part in range(PARTS):
+                for col in range(PIXEL_COLS):
                     turned = turned_pool.tile([P, PASSES, 2, P], F32)
                     for g in range(PASSES):
                         for u in range(2):
                             nc.tensor.transpose(
-                                turned[:, g, u, :], x_sorted[:, part, col, g, u, :], identity[:]
+                                turned[:, g, u, :], x_sorted[:, part, col * PASSES + g, u, :], identity[:]
                             )
                     nc.scalar.copy(
-                        out=grouped_words[:, col, part],
+                        out=grouped_words[:, part, col],
                         in_=turned[:].rearrange("p g u b -> p g b u"),
                     )
             return grouped
 
         def quantise(r, grouped):
-            codes = mx_pool.tile([P, PIXEL_COLS, PARTS, PASSES, P], U32, align_bytes=64)
-            planes = mx_pool.tile([P, PIXEL_COLS, PARTS, PASSES, P], U8, align_bytes=64)
-            for col in range(PIXEL_COLS):
+            codes = mx_pool.tile([P, PARTS, PIXEL_COLS, PASSES, P], U32, align_bytes=64)
+            planes = mx_pool.tile([P, PARTS, PIXEL_COLS, PASSES, P], U8, align_bytes=64)
+            for part in range(PARTS):
                 nc.vector.quantize_mx(
-                    out=codes[:, col].rearrange("p a g b -> p (a g b)").bitcast(FP8X4),
-                    scales=planes[:, col].rearrange("p a g b -> p (a g b)"),
-                    in_=grouped[:, col].rearrange("p a g b t -> p (a g b t)"),
+                    out=codes[:, part].rearrange("p w g b -> p (w g b)").bitcast(FP8X4),
+                    scales=planes[:, part].rearrange("p w g b -> p (w g b)"),
+                    in_=grouped[:, part].rearrange("p w g b t -> p (w g b t)"),
                 )
             quantised[r] = (codes, planes)
 
@@ -145,8 +141,8 @@ def tile_dot_pa_t_e_kernel(
                 for n, (x_part, w_part, g) in enumerate(passes):
                     nc.tensor.matmul_mx(
                         out=acc[:, col, :],
-                        lhsT=codes[:, col, x_part, g, :].bitcast(FP8X4),
-                        lhsT_scale=planes[:, col, x_part, g, :],
+                        lhsT=codes[:, x_part, col, g, :].bitcast(FP8X4),
+                        lhsT_scale=planes[:, x_part, col, g, :],
                         rhs=w_words[:, w_part, pixel * PASSES + g, :].bitcast(FP8X4),
                         rhs_scale=w_planes[:, w_part, pixel * PASSES + g, :],
                         start=(n == 0),
@@ -159,26 +155,31 @@ def tile_dot_pa_t_e_kernel(
                 group(im, col, [(REAL, IMAG), (IMAG, REAL)])
             for col in range(PIXEL_COLS):
                 group(ii, col, [(IMAG, IMAG)])
-            sums[r] = (rr, ii, im)
+            sums[r] = (rr, im, ii)
 
         def add_up(r):
-            rr, ii, im = sums[r]
+            rr, im, ii = sums[r]
             shape = [P, PIXEL_COLS, FEATURES]
             rr_biased = out_pool.tile(shape, F32)
             y = out_pool.tile([P, PARTS, PIXEL_COLS, FEATURES], F32)
             nc.vector.tensor_tensor(
-                out=rr_biased[:], in0=rr[:], in1=bias[:, REAL : REAL + 1, :].to_broadcast(shape), op=ADD
+                out=rr_biased[:], in0=rr[:], in1=bias[:, REAL : REAL + 1, :].to_broadcast(shape), op=ALU.add
             )
             nc.vector.tensor_tensor(
-                out=y[:, IMAG], in0=im[:], in1=bias[:, IMAG : IMAG + 1, :].to_broadcast(shape), op=ADD
+                out=y[:, IMAG], in0=im[:], in1=bias[:, IMAG : IMAG + 1, :].to_broadcast(shape), op=ALU.add
             )
-            nc.vector.tensor_tensor(out=y[:, REAL], in0=rr_biased[:], in1=ii[:], op=SUBTRACT)
+            nc.vector.tensor_tensor(out=y[:, REAL], in0=rr_biased[:], in1=ii[:], op=ALU.subtract)
             before_relu[r] = y
 
         def relu_and_store(r):
+            y = before_relu[r]
             result = out_pool.tile([P, PARTS, PIXEL_COLS, FEATURES], F32)
-            nc.scalar.activation(out=result[:], in_=before_relu[r][:], func=RELU)
-            nc.sync.dma_start(out=out[rows_of(r), :, r % PIXEL_ROWS, :, :], in_=result[:])
+            for part in (IMAG, REAL):
+                nc.gpsimd.tensor_scalar(
+                    out=result[:, part], in0=y[:, part],
+                    scalar1=LARGEST_F32, scalar2=0.0, op0=ALU.min, op1=ALU.max,
+                )
+                nc.sync.dma_start(out=out[rows_of(r), part, r % PIXEL_ROWS, :, :], in_=result[:, part])
 
         load_x(0)
         load_x(1)
@@ -188,19 +189,18 @@ def tile_dot_pa_t_e_kernel(
         load_weight_words(1)
         load_x(3)
 
-        for r in range(SORT_AHEAD):
-            sort_words(r)
-            load_x(r + X_BUFS)
+        sort_words(0)
+        load_x(X_BUFS)
 
         for step in range(ROUNDS + 2):
             if step < ROUNDS:
                 grouped = transpose(step)
             if step >= 2:
                 add_up(step - 2)
-            if step + SORT_AHEAD < ROUNDS:
-                sort_words(step + SORT_AHEAD)
-            if step + SORT_AHEAD + X_BUFS < ROUNDS:
-                load_x(step + SORT_AHEAD + X_BUFS)
+            if step + 1 < ROUNDS:
+                sort_words(step + 1)
+            if step + 1 + X_BUFS < ROUNDS:
+                load_x(step + 1 + X_BUFS)
             if step < ROUNDS:
                 quantise(step, grouped)
             if 1 <= step <= ROUNDS:

@@ -10,6 +10,7 @@ U32 = mybir.dt.uint32
 U8 = mybir.dt.uint8
 FP8X4 = mybir.dt.float8_e4m3fn_x4
 ALU = mybir.AluOpType
+RELU = mybir.ActivationFunctionType.Relu
 
 P = 128
 PACK = 4
@@ -17,10 +18,10 @@ BATCH, PARTS, PIXEL_ROWS, PIXEL_COLS, CHANNELS = 1024, 2, 2, 2, 1024
 FEATURES = 256
 REAL, IMAG = 0, 1
 PASSES = CHANNELS // (P * PACK)
-WEIGHT_GROUPS = PIXEL_ROWS * PIXEL_COLS * PASSES
-ROUNDS = (BATCH // P) * PIXEL_ROWS
+ROW_GROUPS = PIXEL_COLS * PASSES
+BATCH_TILES = BATCH // P
+ROUNDS = BATCH_TILES * PIXEL_ROWS
 X_BUFS = 4
-LARGEST_F32 = 3.4028234663852886e38
 
 FLOPS = 2 * 4 * BATCH * PIXEL_ROWS * PIXEL_COLS * CHANNELS * FEATURES
 
@@ -33,22 +34,41 @@ def tile_dot_pa_t_e_kernel(
         const = ctx.enter_context(tc.tile_pool(name="const", bufs=1))
         x_pool = ctx.enter_context(tc.tile_pool(name="x", bufs=X_BUFS))
         mx_pool = ctx.enter_context(tc.tile_pool(name="mx", bufs=2))
-        out_pool = ctx.enter_context(tc.tile_pool(name="out", bufs=3))
+        out_pool = ctx.enter_context(tc.tile_pool(name="out", bufs=2))
         turned_pool = ctx.enter_context(tc.psum_pool(name="turned", bufs=4))
         sum_pool = ctx.enter_context(tc.psum_pool(name="sums", bufs=4))
         ctx.enter_context(tc.manual_schedule())
 
+        def pixel_row_of(r):
+            return r // BATCH_TILES
+
         def rows_of(r):
-            return slice((r // PIXEL_ROWS) * P, (r // PIXEL_ROWS + 1) * P)
+            return slice((r % BATCH_TILES) * P, (r % BATCH_TILES + 1) * P)
 
         identity = const.tile([P, P], F32)
         make_identity(nc, identity[:])
-        w_words = const.tile([P, PARTS, WEIGHT_GROUPS, FEATURES], U32, align_bytes=64)
-        w_planes = const.tile([P, PARTS, WEIGHT_GROUPS, FEATURES], U8, align_bytes=64)
-        nc.vector.memset(w_planes[:].rearrange("p a g n -> p (a g n)").bitcast(I32), 0)
-        bias = const.tile([P, PARTS, FEATURES], BF16)
-        nc.scalar.dma_start(out=bias[:, REAL, :], in_=b_r.partition_broadcast(P))
-        nc.scalar.dma_start(out=bias[:, IMAG, :], in_=b_i.partition_broadcast(P))
+        w_words = const.tile([P, PARTS, PIXEL_ROWS, ROW_GROUPS, FEATURES], U32, align_bytes=64)
+        w_planes = const.tile([P, PARTS, PIXEL_ROWS, FEATURES], U8, align_bytes=64)
+        nc.vector.memset(w_planes[:].rearrange("p a h n -> p (a h n)").bitcast(I32), 0)
+
+        ones = const.tile([P, P], BF16)
+        nc.vector.memset(ones[:], 1.0)
+        bias_rows = const.tile([P, PARTS, FEATURES], BF16)
+        nc.vector.memset(bias_rows[:], 0.0)
+        nc.scalar.dma_start(out=bias_rows[0:1, REAL, :], in_=b_r.unsqueeze(0))
+        nc.scalar.dma_start(out=bias_rows[0:1, IMAG, :], in_=b_i.unsqueeze(0))
+        bias_spread = sum_pool.tile([P, PARTS, FEATURES], F32, tag="sum")
+        nc.tensor.matmul(
+            out=bias_spread[:].rearrange("p a n -> p (a n)"),
+            lhsT=ones[:],
+            rhs=bias_rows[:].rearrange("p a n -> p (a n)"),
+            start=True,
+            stop=True,
+        )
+        bias = const.tile([P, PARTS, FEATURES], F32)
+        nc.vector.tensor_copy(out=bias[:], in_=bias_spread[:])
+        table_warmer = const.tile([P, 1], F32)
+        nc.scalar.activation(out=table_warmer[:], in_=ones[:, 0:1], func=RELU)
 
         x_tiles = {}
         sorted_tiles = {}
@@ -60,26 +80,22 @@ def tile_dot_pa_t_e_kernel(
             x_sb = x_pool.tile([P, PARTS, PIXEL_COLS, CHANNELS], BF16)
             for part in range(PARTS):
                 nc.sync.dma_start(
-                    out=x_sb[:, part], in_=x_crop[rows_of(r), part, r % PIXEL_ROWS, :, :]
+                    out=x_sb[:, part], in_=x_crop[rows_of(r), part, pixel_row_of(r), :, :]
                 )
             x_tiles[r] = x_sb
 
-        def load_weight_scales():
+        def load_weights(pixel_row):
+            groups = slice(pixel_row * ROW_GROUPS, (pixel_row + 1) * ROW_GROUPS)
             for part, scales in enumerate((W_r_scales, W_i_scales)):
-                by_row = scales.bitcast(I32).rearrange("g (q j) n -> j q g n", j=4)
-                for j in range(4):
+                for quadrant in range(4):
                     nc.sync.dma_start(
-                        out=w_planes[j:P:32, part, :, :].bitcast(I32), in_=by_row[j]
+                        out=w_planes[32 * quadrant : 32 * quadrant + 16, part, pixel_row, :].bitcast(I32),
+                        in_=scales.bitcast(I32)[groups, 4 * quadrant : 4 * quadrant + 4, :],
                     )
-
-        def load_weight_words(pixel_row):
-            groups = slice(
-                pixel_row * PIXEL_COLS * PASSES, (pixel_row + 1) * PIXEL_COLS * PASSES
-            )
             for part, words in enumerate((W_r_words, W_i_words)):
                 as_words = words.rearrange("g p n t -> g p (n t)").bitcast(I32)
                 nc.sync.dma_start(
-                    out=w_words[:, part, groups, :].bitcast(I32),
+                    out=w_words[:, part, pixel_row].bitcast(I32),
                     in_=as_words[groups].rearrange("g p n -> p g n"),
                 )
 
@@ -88,11 +104,12 @@ def tile_dot_pa_t_e_kernel(
                 x_tiles[r][:]
                 .rearrange("p a w c -> p (a w c)")
                 .bitcast(F32)
-                .rearrange("p (a s q u) -> p a s u q", a=PARTS, q=P, u=2)
+                .rearrange("p (a w g q u) -> p a w g u q", a=PARTS, w=PIXEL_COLS, g=PASSES, u=2)
             )
-            x_sorted = mx_pool.tile([P, PARTS, PIXEL_COLS * PASSES, 2, P], F32)
+            x_sorted = mx_pool.tile([P, PARTS, PIXEL_COLS, PASSES, 2, P], F32)
             nc.vector.tensor_copy(out=x_sorted[:, REAL], in_=x_words[:, REAL])
-            nc.scalar.copy(out=x_sorted[:, IMAG], in_=x_words[:, IMAG])
+            nc.vector.tensor_copy(out=x_sorted[:, IMAG, 0], in_=x_words[:, IMAG, 0])
+            nc.scalar.copy(out=x_sorted[:, IMAG, 1], in_=x_words[:, IMAG, 1])
             sorted_tiles[r] = x_sorted
 
         def transpose(r):
@@ -110,7 +127,7 @@ def tile_dot_pa_t_e_kernel(
                     for g in range(PASSES):
                         for u in range(2):
                             nc.tensor.transpose(
-                                turned[:, g, u, :], x_sorted[:, part, col * PASSES + g, u, :], identity[:]
+                                turned[:, g, u, :], x_sorted[:, part, col, g, u, :], identity[:]
                             )
                     nc.scalar.copy(
                         out=grouped_words[:, part, col],
@@ -131,20 +148,21 @@ def tile_dot_pa_t_e_kernel(
 
         def multiply(r):
             codes, planes = quantised[r]
+            pixel_row = pixel_row_of(r)
             rr = sum_pool.tile([P, PIXEL_COLS, FEATURES], F32, tag="sum")
             im = sum_pool.tile([P, PIXEL_COLS, FEATURES], F32, tag="sum")
             ii = sum_pool.tile([P, PIXEL_COLS, FEATURES], F32, tag="sum")
 
             def group(acc, col, products):
-                pixel = (r % PIXEL_ROWS) * PIXEL_COLS + col
                 passes = [(x_part, w_part, g) for x_part, w_part in products for g in range(PASSES)]
                 for n, (x_part, w_part, g) in enumerate(passes):
+                    row_group = col * PASSES + g
                     nc.tensor.matmul_mx(
                         out=acc[:, col, :],
                         lhsT=codes[:, x_part, col, g, :].bitcast(FP8X4),
                         lhsT_scale=planes[:, x_part, col, g, :],
-                        rhs=w_words[:, w_part, pixel * PASSES + g, :].bitcast(FP8X4),
-                        rhs_scale=w_planes[:, w_part, pixel * PASSES + g, :],
+                        rhs=w_words[:, w_part, pixel_row, row_group, :].bitcast(FP8X4),
+                        rhs_scale=w_planes[4 * row_group : P, w_part, pixel_row, :],
                         start=(n == 0),
                         stop=(n == len(passes) - 1),
                     )
@@ -172,25 +190,24 @@ def tile_dot_pa_t_e_kernel(
             before_relu[r] = y
 
         def relu_and_store(r):
-            y = before_relu[r]
             result = out_pool.tile([P, PARTS, PIXEL_COLS, FEATURES], F32)
-            for part in (IMAG, REAL):
-                nc.gpsimd.tensor_scalar(
-                    out=result[:, part], in0=y[:, part],
-                    scalar1=LARGEST_F32, scalar2=0.0, op0=ALU.min, op1=ALU.max,
-                )
-                nc.sync.dma_start(out=out[rows_of(r), part, r % PIXEL_ROWS, :, :], in_=result[:, part])
+            nc.scalar.activation(out=result[:], in_=before_relu[r][:], func=RELU)
+            nc.sync.dma_start(out=out[rows_of(r), :, pixel_row_of(r), :, :], in_=result[:])
+
+        def refill(r):
+            if r < ROUNDS:
+                if r % BATCH_TILES == 0:
+                    load_weights(pixel_row_of(r))
+                load_x(r)
 
         load_x(0)
         load_x(1)
-        load_weight_scales()
-        load_weight_words(0)
+        load_weights(0)
         load_x(2)
-        load_weight_words(1)
         load_x(3)
 
         sort_words(0)
-        load_x(X_BUFS)
+        refill(X_BUFS)
 
         for step in range(ROUNDS + 2):
             if step < ROUNDS:
@@ -199,8 +216,7 @@ def tile_dot_pa_t_e_kernel(
                 add_up(step - 2)
             if step + 1 < ROUNDS:
                 sort_words(step + 1)
-            if step + 1 + X_BUFS < ROUNDS:
-                load_x(step + 1 + X_BUFS)
+                refill(step + 1 + X_BUFS)
             if step < ROUNDS:
                 quantise(step, grouped)
             if 1 <= step <= ROUNDS:

@@ -34,7 +34,7 @@ def tile_dot_pa_t_e_kernel(
         const = ctx.enter_context(tc.tile_pool(name="const", bufs=1))
         x_pool = ctx.enter_context(tc.tile_pool(name="x", bufs=X_BUFS))
         mx_pool = ctx.enter_context(tc.tile_pool(name="mx", bufs=2))
-        out_pool = ctx.enter_context(tc.tile_pool(name="out", bufs=2))
+        out_pool = ctx.enter_context(tc.tile_pool(name="out", bufs=4))
         turned_pool = ctx.enter_context(tc.psum_pool(name="turned", bufs=4))
         sum_pool = ctx.enter_context(tc.psum_pool(name="sums", bufs=4))
         ctx.enter_context(tc.manual_schedule())
@@ -57,16 +57,19 @@ def tile_dot_pa_t_e_kernel(
         nc.vector.memset(bias_rows[:], 0.0)
         nc.scalar.dma_start(out=bias_rows[0:1, REAL, :], in_=b_r.unsqueeze(0))
         nc.scalar.dma_start(out=bias_rows[0:1, IMAG, :], in_=b_i.unsqueeze(0))
-        bias_spread = sum_pool.tile([P, PARTS, FEATURES], F32, tag="sum")
-        nc.tensor.matmul(
-            out=bias_spread[:].rearrange("p a n -> p (a n)"),
-            lhsT=ones[:],
-            rhs=bias_rows[:].rearrange("p a n -> p (a n)"),
-            start=True,
-            stop=True,
-        )
         bias = const.tile([P, PARTS, FEATURES], F32)
-        nc.vector.tensor_copy(out=bias[:], in_=bias_spread[:])
+
+        def spread_bias():
+            bias_spread = sum_pool.tile([P, PARTS, FEATURES], F32, tag="sum")
+            nc.tensor.matmul(
+                out=bias_spread[:].rearrange("p a n -> p (a n)"),
+                lhsT=ones[:],
+                rhs=bias_rows[:].rearrange("p a n -> p (a n)"),
+                start=True,
+                stop=True,
+            )
+            nc.vector.tensor_copy(out=bias[:], in_=bias_spread[:])
+
         table_warmer = const.tile([P, 1], F32)
         nc.scalar.activation(out=table_warmer[:], in_=ones[:, 0:1], func=RELU)
 
@@ -191,8 +194,15 @@ def tile_dot_pa_t_e_kernel(
 
         def relu_and_store(r):
             result = out_pool.tile([P, PARTS, PIXEL_COLS, FEATURES], F32)
-            nc.scalar.activation(out=result[:], in_=before_relu[r][:], func=RELU)
-            nc.sync.dma_start(out=out[rows_of(r), :, pixel_row_of(r), :, :], in_=result[:])
+            if r < ROUNDS - 1:
+                nc.scalar.activation(out=result[:], in_=before_relu[r][:], func=RELU)
+                nc.sync.dma_start(out=out[rows_of(r), :, pixel_row_of(r), :, :], in_=result[:])
+            else:
+                for part in (IMAG, REAL):
+                    nc.scalar.activation(out=result[:, part], in_=before_relu[r][:, part], func=RELU)
+                    nc.sync.dma_start(
+                        out=out[rows_of(r), part, pixel_row_of(r), :, :], in_=result[:, part]
+                    )
 
         def refill(r):
             if r < ROUNDS:
@@ -219,6 +229,8 @@ def tile_dot_pa_t_e_kernel(
                 refill(step + 1 + X_BUFS)
             if step < ROUNDS:
                 quantise(step, grouped)
+            if step == 0:
+                spread_bias()
             if 1 <= step <= ROUNDS:
                 multiply(step - 1)
             if step >= 2:

@@ -87,20 +87,29 @@ def tile_dot_pa_t_e_kernel(
                 )
             x_tiles[r] = x_sb
 
-        def load_weights(pixel_row):
+        def load_scales(part, pixel_row):
             groups = slice(pixel_row * ROW_GROUPS, (pixel_row + 1) * ROW_GROUPS)
-            for part, scales in enumerate((W_r_scales, W_i_scales)):
-                for quadrant in range(4):
-                    nc.sync.dma_start(
-                        out=w_planes[32 * quadrant : 32 * quadrant + 16, part, pixel_row, :].bitcast(I32),
-                        in_=scales.bitcast(I32)[groups, 4 * quadrant : 4 * quadrant + 4, :],
-                    )
-            for part, words in enumerate((W_r_words, W_i_words)):
-                as_words = words.rearrange("g p n t -> g p (n t)").bitcast(I32)
+            scales = (W_r_scales, W_i_scales)[part]
+            for quadrant in range(4):
                 nc.sync.dma_start(
-                    out=w_words[:, part, pixel_row].bitcast(I32),
-                    in_=as_words[groups].rearrange("g p n -> p g n"),
+                    out=w_planes[32 * quadrant : 32 * quadrant + 16, part, pixel_row, :].bitcast(I32),
+                    in_=scales.bitcast(I32)[groups, 4 * quadrant : 4 * quadrant + 4, :],
                 )
+
+        def load_words(part, pixel_row):
+            groups = slice(pixel_row * ROW_GROUPS, (pixel_row + 1) * ROW_GROUPS)
+            words = (W_r_words, W_i_words)[part]
+            as_words = words.rearrange("g p n t -> g p (n t)").bitcast(I32)
+            nc.sync.dma_start(
+                out=w_words[:, part, pixel_row].bitcast(I32),
+                in_=as_words[groups].rearrange("g p n -> p g n"),
+            )
+
+        def load_weights(pixel_row):
+            for part in range(PARTS):
+                load_scales(part, pixel_row)
+            for part in range(PARTS):
+                load_words(part, pixel_row)
 
         def sort_words(r):
             x_words = (
@@ -211,8 +220,11 @@ def tile_dot_pa_t_e_kernel(
                 load_x(r)
 
         load_x(0)
+        load_scales(REAL, 0)
         load_x(1)
-        load_weights(0)
+        load_words(REAL, 0)
+        load_scales(IMAG, 0)
+        load_words(IMAG, 0)
         load_x(2)
         load_x(3)
 

@@ -112,16 +112,17 @@ def tile_dot_pa_t_e_kernel(
                 load_words(part, pixel_row)
 
         def sort_words(r):
-            x_words = (
+            x_blocks = (
                 x_tiles[r][:]
                 .rearrange("p a w c -> p (a w c)")
                 .bitcast(F32)
-                .rearrange("p (a w g q u) -> p a w g u q", a=PARTS, w=PIXEL_COLS, g=PASSES, u=2)
+                .rearrange("p (k c i u) -> p k c u i", k=PARTS * PIXEL_COLS * PASSES, i=4, u=2)
             )
-            x_sorted = mx_pool.tile([P, PARTS, PIXEL_COLS, PASSES, 2, P], F32)
-            nc.vector.tensor_copy(out=x_sorted[:, REAL], in_=x_words[:, REAL])
-            nc.vector.tensor_copy(out=x_sorted[:, IMAG, 0], in_=x_words[:, IMAG, 0])
-            nc.scalar.copy(out=x_sorted[:, IMAG, 1], in_=x_words[:, IMAG, 1])
+            x_sorted = mx_pool.tile([P, 2, PARTS, PIXEL_COLS, PASSES, P], F32)
+            sorted_blocks = x_sorted[:].rearrange("p u a w g (c i) -> p (a w g) c u i", i=4)
+            nc.vector.tensor_copy(out=sorted_blocks[:, 0:4], in_=x_blocks[:, 0:4])
+            nc.vector.tensor_copy(out=sorted_blocks[:, 4:6], in_=x_blocks[:, 4:6])
+            nc.scalar.copy(out=sorted_blocks[:, 6:8], in_=x_blocks[:, 6:8])
             sorted_tiles[r] = x_sorted
 
         def transpose(r):
@@ -139,7 +140,7 @@ def tile_dot_pa_t_e_kernel(
                     for g in range(PASSES):
                         for u in range(2):
                             nc.tensor.transpose(
-                                turned[:, g, u, :], x_sorted[:, part, col, g, u, :], identity[:]
+                                turned[:, g, u, :], x_sorted[:, u, part, col, g, :], identity[:]
                             )
                     nc.scalar.copy(
                         out=grouped_words[:, part, col],

@@ -39,11 +39,16 @@ def tile_dot_pa_t_e_kernel(
         sum_pool = ctx.enter_context(tc.psum_pool(name="sums", bufs=4))
         ctx.enter_context(tc.manual_schedule())
 
-        def pixel_row_of(r):
-            return r // BATCH_TILES
+        units = []
+        for tile_index in range(ROUNDS):
+            pixel_row, batch_tile = divmod(tile_index, BATCH_TILES)
+            if tile_index in (0, ROUNDS - 1):
+                units.extend((pixel_row, batch_tile, col, 1) for col in range(PIXEL_COLS))
+            else:
+                units.append((pixel_row, batch_tile, 0, PIXEL_COLS))
 
-        def rows_of(r):
-            return slice((r % BATCH_TILES) * P, (r % BATCH_TILES + 1) * P)
+        def rows_of(batch_tile):
+            return slice(batch_tile * P, (batch_tile + 1) * P)
 
         identity = const.tile([P, P], F32)
         make_identity(nc, identity[:])
@@ -55,8 +60,8 @@ def tile_dot_pa_t_e_kernel(
         nc.vector.memset(ones[:], 1.0)
         bias_rows = const.tile([P, PARTS, FEATURES], BF16)
         nc.vector.memset(bias_rows[:], 0.0)
-        nc.scalar.dma_start(out=bias_rows[0:1, REAL, :], in_=b_r.unsqueeze(0))
-        nc.scalar.dma_start(out=bias_rows[0:1, IMAG, :], in_=b_i.unsqueeze(0))
+        nc.gpsimd.dma_start(out=bias_rows[0:1, REAL, :], in_=b_r.unsqueeze(0))
+        nc.gpsimd.dma_start(out=bias_rows[0:1, IMAG, :], in_=b_i.unsqueeze(0))
         bias = const.tile([P, PARTS, FEATURES], F32)
 
         def spread_bias():
@@ -79,13 +84,18 @@ def tile_dot_pa_t_e_kernel(
         sums = {}
         before_relu = {}
 
-        def load_x(r):
+        def load_x(tile_index):
+            pixel_row, batch_tile = divmod(tile_index, BATCH_TILES)
             x_sb = x_pool.tile([P, PARTS, PIXEL_COLS, CHANNELS], BF16)
-            for part in range(PARTS):
-                nc.sync.dma_start(
-                    out=x_sb[:, part], in_=x_crop[rows_of(r), part, pixel_row_of(r), :, :]
-                )
-            x_tiles[r] = x_sb
+            x_tiles[tile_index] = x_sb
+            if tile_index > 0:
+                for part in range(PARTS):
+                    nc.sync.dma_start(
+                        out=x_sb[:, part], in_=x_crop[rows_of(batch_tile), part, pixel_row, :, :]
+                    )
+
+        def load_x_column(col):
+            nc.sync.dma_start(out=x_tiles[0][:, :, col, :], in_=x_crop[rows_of(0), :, 0, col, :])
 
         def load_scales(part, pixel_row):
             groups = slice(pixel_row * ROW_GROUPS, (pixel_row + 1) * ROW_GROUPS)
@@ -96,12 +106,13 @@ def tile_dot_pa_t_e_kernel(
                     in_=scales.bitcast(I32)[groups, 4 * quadrant : 4 * quadrant + 4, :],
                 )
 
-        def load_words(part, pixel_row):
-            groups = slice(pixel_row * ROW_GROUPS, (pixel_row + 1) * ROW_GROUPS)
+        def load_words(part, pixel_row, first_group=0, n_groups=ROW_GROUPS):
+            row_groups = slice(first_group, first_group + n_groups)
+            groups = slice(pixel_row * ROW_GROUPS + first_group, pixel_row * ROW_GROUPS + first_group + n_groups)
             words = (W_r_words, W_i_words)[part]
             as_words = words.rearrange("g p n t -> g p (n t)").bitcast(I32)
             nc.sync.dma_start(
-                out=w_words[:, part, pixel_row].bitcast(I32),
+                out=w_words[:, part, pixel_row, row_groups].bitcast(I32),
                 in_=as_words[groups].rearrange("g p n -> p g n"),
             )
 
@@ -111,31 +122,38 @@ def tile_dot_pa_t_e_kernel(
             for part in range(PARTS):
                 load_words(part, pixel_row)
 
-        def sort_words(r):
-            x_blocks = (
-                x_tiles[r][:]
-                .rearrange("p a w c -> p (a w c)")
-                .bitcast(F32)
-                .rearrange("p (k c i u) -> p k c u i", k=PARTS * PIXEL_COLS * PASSES, i=4, u=2)
-            )
-            x_sorted = mx_pool.tile([P, 2, PARTS, PIXEL_COLS, PASSES, P], F32)
-            sorted_blocks = x_sorted[:].rearrange("p u a w g (c i) -> p (a w g) c u i", i=4)
-            nc.vector.tensor_copy(out=sorted_blocks[:, 0:4], in_=x_blocks[:, 0:4])
-            nc.vector.tensor_copy(out=sorted_blocks[:, 4:6], in_=x_blocks[:, 4:6])
-            nc.scalar.copy(out=sorted_blocks[:, 6:8], in_=x_blocks[:, 6:8])
-            sorted_tiles[r] = x_sorted
+        def sort_words(s):
+            pixel_row, batch_tile, first_col, cols = units[s]
+            x_sb = x_tiles[pixel_row * BATCH_TILES + batch_tile]
+            x_sorted = mx_pool.tile([P, 2, PARTS, cols, PASSES, P], F32)
 
-        def transpose(r):
-            x_sorted = sorted_tiles[r]
-            grouped = mx_pool.tile([P, PARTS, PIXEL_COLS, PASSES, P, PACK], BF16, align_bytes=64)
+            def sort(copy, part, lo, hi):
+                copy(
+                    out=x_sorted[:, :, part, lo:hi].rearrange("p u w g (c i) -> p (w g) c u i", i=4),
+                    in_=x_sb[:, part, first_col + lo : first_col + hi]
+                    .rearrange("p w c -> p (w c)")
+                    .bitcast(F32)
+                    .rearrange("p (k c i u) -> p k c u i", k=(hi - lo) * PASSES, i=4, u=2),
+                )
+
+            sort(nc.vector.tensor_copy, REAL, 0, cols)
+            sort(nc.vector.tensor_copy, IMAG, 0, 1)
+            if cols > 1:
+                sort(nc.scalar.copy, IMAG, 1, cols)
+            sorted_tiles[s] = x_sorted
+
+        def transpose(s):
+            cols = units[s][3]
+            x_sorted = sorted_tiles[s]
+            grouped = mx_pool.tile([P, PARTS, cols, PASSES, P, PACK], BF16, align_bytes=64)
             grouped_words = (
                 grouped[:]
                 .rearrange("p a w g b t -> p (a w g b t)")
                 .bitcast(F32)
-                .rearrange("p (a w g b u) -> p a w g b u", a=PARTS, w=PIXEL_COLS, g=PASSES, u=2)
+                .rearrange("p (a w g b u) -> p a w g b u", a=PARTS, w=cols, g=PASSES, u=2)
             )
             for part in range(PARTS):
-                for col in range(PIXEL_COLS):
+                for col in range(cols):
                     turned = turned_pool.tile([P, PASSES, 2, P], F32)
                     for g in range(PASSES):
                         for u in range(2):
@@ -148,28 +166,29 @@ def tile_dot_pa_t_e_kernel(
                     )
             return grouped
 
-        def quantise(r, grouped):
-            codes = mx_pool.tile([P, PARTS, PIXEL_COLS, PASSES, P], U32, align_bytes=64)
-            planes = mx_pool.tile([P, PARTS, PIXEL_COLS, PASSES, P], U8, align_bytes=64)
+        def quantise(s, grouped):
+            cols = units[s][3]
+            codes = mx_pool.tile([P, PARTS, cols, PASSES, P], U32, align_bytes=64)
+            planes = mx_pool.tile([P, PARTS, cols, PASSES, P], U8, align_bytes=64)
             for part in range(PARTS):
                 nc.vector.quantize_mx(
                     out=codes[:, part].rearrange("p w g b -> p (w g b)").bitcast(FP8X4),
                     scales=planes[:, part].rearrange("p w g b -> p (w g b)"),
                     in_=grouped[:, part].rearrange("p w g b t -> p (w g b t)"),
                 )
-            quantised[r] = (codes, planes)
+            quantised[s] = (codes, planes)
 
-        def multiply(r):
-            codes, planes = quantised[r]
-            pixel_row = pixel_row_of(r)
-            rr = sum_pool.tile([P, PIXEL_COLS, FEATURES], F32, tag="sum")
-            im = sum_pool.tile([P, PIXEL_COLS, FEATURES], F32, tag="sum")
-            ii = sum_pool.tile([P, PIXEL_COLS, FEATURES], F32, tag="sum")
+        def multiply(s):
+            codes, planes = quantised[s]
+            pixel_row, batch_tile, first_col, cols = units[s]
+            rr = sum_pool.tile([P, cols, FEATURES], F32, tag="sum")
+            im = sum_pool.tile([P, cols, FEATURES], F32, tag="sum")
+            ii = sum_pool.tile([P, cols, FEATURES], F32, tag="sum")
 
             def group(acc, col, products):
                 passes = [(x_part, w_part, g) for x_part, w_part in products for g in range(PASSES)]
                 for n, (x_part, w_part, g) in enumerate(passes):
-                    row_group = col * PASSES + g
+                    row_group = (first_col + col) * PASSES + g
                     nc.tensor.matmul_mx(
                         out=acc[:, col, :],
                         lhsT=codes[:, x_part, col, g, :].bitcast(FP8X4),
@@ -180,19 +199,20 @@ def tile_dot_pa_t_e_kernel(
                         stop=(n == len(passes) - 1),
                     )
 
-            for col in range(PIXEL_COLS):
+            for col in range(cols):
                 group(rr, col, [(REAL, REAL)])
-            for col in range(PIXEL_COLS):
+            for col in range(cols):
                 group(im, col, [(REAL, IMAG), (IMAG, REAL)])
-            for col in range(PIXEL_COLS):
+            for col in range(cols):
                 group(ii, col, [(IMAG, IMAG)])
-            sums[r] = (rr, im, ii)
+            sums[s] = (rr, im, ii)
 
-        def add_up(r):
-            rr, im, ii = sums[r]
-            shape = [P, PIXEL_COLS, FEATURES]
+        def add_up(s):
+            cols = units[s][3]
+            rr, im, ii = sums[s]
+            shape = [P, cols, FEATURES]
             rr_biased = out_pool.tile(shape, F32)
-            y = out_pool.tile([P, PARTS, PIXEL_COLS, FEATURES], F32)
+            y = out_pool.tile([P, PARTS, cols, FEATURES], F32)
             nc.vector.tensor_tensor(
                 out=rr_biased[:], in0=rr[:], in1=bias[:, REAL : REAL + 1, :].to_broadcast(shape), op=ALU.add
             )
@@ -200,51 +220,61 @@ def tile_dot_pa_t_e_kernel(
                 out=y[:, IMAG], in0=im[:], in1=bias[:, IMAG : IMAG + 1, :].to_broadcast(shape), op=ALU.add
             )
             nc.vector.tensor_tensor(out=y[:, REAL], in0=rr_biased[:], in1=ii[:], op=ALU.subtract)
-            before_relu[r] = y
+            before_relu[s] = y
 
-        def relu_and_store(r):
-            result = out_pool.tile([P, PARTS, PIXEL_COLS, FEATURES], F32)
-            if r < ROUNDS - 1:
-                nc.scalar.activation(out=result[:], in_=before_relu[r][:], func=RELU)
-                nc.sync.dma_start(out=out[rows_of(r), :, pixel_row_of(r), :, :], in_=result[:])
+        def relu_and_store(s):
+            pixel_row, batch_tile, first_col, cols = units[s]
+            result = out_pool.tile([P, PARTS, cols, FEATURES], F32)
+            columns = slice(first_col, first_col + cols)
+            if s < len(units) - 1:
+                nc.scalar.activation(out=result[:], in_=before_relu[s][:], func=RELU)
+                nc.sync.dma_start(out=out[rows_of(batch_tile), :, pixel_row, columns, :], in_=result[:])
             else:
                 for part in (IMAG, REAL):
-                    nc.scalar.activation(out=result[:, part], in_=before_relu[r][:, part], func=RELU)
+                    nc.scalar.activation(out=result[:, part], in_=before_relu[s][:, part], func=RELU)
                     nc.sync.dma_start(
-                        out=out[rows_of(r), part, pixel_row_of(r), :, :], in_=result[:, part]
+                        out=out[rows_of(batch_tile), part, pixel_row, columns, :], in_=result[:, part]
                     )
 
-        def refill(r):
-            if r < ROUNDS:
-                if r % BATCH_TILES == 0:
-                    load_weights(pixel_row_of(r))
-                load_x(r)
+        def refill(s):
+            pixel_row, batch_tile, first_col, cols = units[s]
+            if first_col + cols == PIXEL_COLS:
+                tile_index = pixel_row * BATCH_TILES + batch_tile + X_BUFS
+                if tile_index < ROUNDS:
+                    if tile_index % BATCH_TILES == 0:
+                        load_weights(tile_index // BATCH_TILES)
+                    load_x(tile_index)
 
         load_x(0)
+        load_x_column(0)
         load_scales(REAL, 0)
-        load_x(1)
-        load_words(REAL, 0)
+        load_x_column(1)
+        load_words(REAL, 0, 0, PASSES)
+        load_words(IMAG, 0, 0, PASSES)
         load_scales(IMAG, 0)
-        load_words(IMAG, 0)
+        load_x(1)
+        load_words(REAL, 0, PASSES, PASSES)
+        load_words(IMAG, 0, PASSES, PASSES)
         load_x(2)
         load_x(3)
 
         sort_words(0)
-        refill(X_BUFS)
+        refill(0)
 
-        for step in range(ROUNDS + 2):
-            if step < ROUNDS:
+        count = len(units)
+        for step in range(count + 2):
+            if step < count:
                 grouped = transpose(step)
             if step >= 2:
                 add_up(step - 2)
-            if step + 1 < ROUNDS:
+            if step + 1 < count:
                 sort_words(step + 1)
-                refill(step + 1 + X_BUFS)
-            if step < ROUNDS:
+                refill(step + 1)
+            if step < count:
                 quantise(step, grouped)
-            if step == 0:
+            if step == 1:
                 spread_bias()
-            if 1 <= step <= ROUNDS:
+            if 1 <= step <= count:
                 multiply(step - 1)
             if step >= 2:
                 relu_and_store(step - 2)

@@ -21,7 +21,7 @@ PASSES = CHANNELS // (P * PACK)
 ROW_GROUPS = PIXEL_COLS * PASSES
 BATCH_TILES = BATCH // P
 ROUNDS = BATCH_TILES * PIXEL_ROWS
-X_BUFS = 4
+X_BUFS = 10
 
 FLOPS = 2 * 4 * BATCH * PIXEL_ROWS * PIXEL_COLS * CHANNELS * FEATURES
 
@@ -239,11 +239,13 @@ def tile_dot_pa_t_e_kernel(
         def refill(s):
             pixel_row, batch_tile, first_col, cols = units[s]
             if first_col + cols == PIXEL_COLS:
-                tile_index = pixel_row * BATCH_TILES + batch_tile + X_BUFS
-                if tile_index < ROUNDS:
-                    if tile_index % BATCH_TILES == 0:
-                        load_weights(tile_index // BATCH_TILES)
-                    load_x(tile_index)
+                load_next(pixel_row * BATCH_TILES + batch_tile + X_BUFS)
+
+        def load_next(tile_index):
+            if tile_index < ROUNDS:
+                if tile_index % BATCH_TILES == 0:
+                    load_weights(tile_index // BATCH_TILES)
+                load_x(tile_index)
 
         load_x(0)
         load_x_column(0)
@@ -255,8 +257,8 @@ def tile_dot_pa_t_e_kernel(
         load_x(1)
         load_words(REAL, 0, PASSES, PASSES)
         load_words(IMAG, 0, PASSES, PASSES)
-        load_x(2)
-        load_x(3)
+        for tile_index in range(2, X_BUFS):
+            load_next(tile_index)
 
         sort_words(0)
         refill(0)

@@ -21,7 +21,7 @@ PASSES = CHANNELS // (P * PACK)
 ROW_GROUPS = PIXEL_COLS * PASSES
 BATCH_TILES = BATCH // P
 ROUNDS = BATCH_TILES * PIXEL_ROWS
-X_BUFS = 10
+X_BUFS = 7
 
 FLOPS = 2 * 4 * BATCH * PIXEL_ROWS * PIXEL_COLS * CHANNELS * FEATURES
 
@@ -34,7 +34,8 @@ def tile_dot_pa_t_e_kernel(
         const = ctx.enter_context(tc.tile_pool(name="const", bufs=1))
         x_pool = ctx.enter_context(tc.tile_pool(name="x", bufs=X_BUFS))
         mx_pool = ctx.enter_context(tc.tile_pool(name="mx", bufs=2))
-        out_pool = ctx.enter_context(tc.tile_pool(name="out", bufs=4))
+        out_pool = ctx.enter_context(tc.tile_pool(name="out", bufs=3))
+        result_pool = ctx.enter_context(tc.tile_pool(name="result", bufs=8))
         turned_pool = ctx.enter_context(tc.psum_pool(name="turned", bufs=4))
         sum_pool = ctx.enter_context(tc.psum_pool(name="sums", bufs=4))
         ctx.enter_context(tc.manual_schedule())
@@ -224,7 +225,7 @@ def tile_dot_pa_t_e_kernel(
 
         def relu_and_store(s):
             pixel_row, batch_tile, first_col, cols = units[s]
-            result = out_pool.tile([P, PARTS, cols, FEATURES], F32)
+            result = result_pool.tile([P, PARTS, cols, FEATURES], F32)
             columns = slice(first_col, first_col + cols)
             if s < len(units) - 1:
                 nc.scalar.activation(out=result[:], in_=before_relu[s][:], func=RELU)

@@ -21,6 +21,7 @@ PASSES = CHANNELS // (P * PACK)
 ROW_GROUPS = PIXEL_COLS * PASSES
 BATCH_TILES = BATCH // P
 ROUNDS = BATCH_TILES * PIXEL_ROWS
+HEAD_TILES = 1
 X_BUFS = 7
 
 FLOPS = 2 * 4 * BATCH * PIXEL_ROWS * PIXEL_COLS * CHANNELS * FEATURES
@@ -40,12 +41,12 @@ def tile_dot_pa_t_e_kernel(
         sum_pool = ctx.enter_context(tc.psum_pool(name="sums", bufs=4))
         ctx.enter_context(tc.manual_schedule())
 
-        units = []
+        units = [(0, batch_tile, col, 1) for col in range(PIXEL_COLS) for batch_tile in range(HEAD_TILES)]
         for tile_index in range(ROUNDS):
             pixel_row, batch_tile = divmod(tile_index, BATCH_TILES)
-            if tile_index in (0, ROUNDS - 1):
+            if tile_index == ROUNDS - 1:
                 units.extend((pixel_row, batch_tile, col, 1) for col in range(PIXEL_COLS))
-            else:
+            elif tile_index >= HEAD_TILES:
                 units.append((pixel_row, batch_tile, 0, PIXEL_COLS))
 
         def rows_of(batch_tile):
@@ -87,16 +88,21 @@ def tile_dot_pa_t_e_kernel(
 
         def load_x(tile_index):
             pixel_row, batch_tile = divmod(tile_index, BATCH_TILES)
-            x_sb = x_pool.tile([P, PARTS, PIXEL_COLS, CHANNELS], BF16)
+            if tile_index < HEAD_TILES:
+                x_sb = x_pool.tile([P, PIXEL_COLS, PARTS, CHANNELS], BF16)
+            else:
+                x_sb = x_pool.tile([P, PARTS, PIXEL_COLS, CHANNELS], BF16)
             x_tiles[tile_index] = x_sb
-            if tile_index > 0:
+            if tile_index >= HEAD_TILES:
                 for part in range(PARTS):
                     nc.sync.dma_start(
                         out=x_sb[:, part], in_=x_crop[rows_of(batch_tile), part, pixel_row, :, :]
                     )
 
-        def load_x_column(col):
-            nc.sync.dma_start(out=x_tiles[0][:, :, col, :], in_=x_crop[rows_of(0), :, 0, col, :])
+        def load_x_column(batch_tile, col):
+            nc.sync.dma_start(
+                out=x_tiles[batch_tile][:, col], in_=x_crop[rows_of(batch_tile), :, 0, col, :]
+            )
 
         def load_scales(part, pixel_row):
             groups = slice(pixel_row * ROW_GROUPS, (pixel_row + 1) * ROW_GROUPS)
@@ -125,27 +131,30 @@ def tile_dot_pa_t_e_kernel(
 
         def sort_words(s):
             pixel_row, batch_tile, first_col, cols = units[s]
-            x_sb = x_tiles[pixel_row * BATCH_TILES + batch_tile]
-            x_sorted = mx_pool.tile([P, 2, PARTS, cols, PASSES, P], F32)
+            tile_index = pixel_row * BATCH_TILES + batch_tile
 
             def sort(copy, part, lo, hi):
+                x_sorted = mx_pool.tile([P, 2, hi - lo, PASSES, P], F32, tag="sorted%d%d" % (part, lo))
+                if tile_index < HEAD_TILES:
+                    x_words = x_tiles[tile_index][:, first_col, part]
+                else:
+                    x_words = x_tiles[tile_index][:, part, first_col + lo : first_col + hi].rearrange(
+                        "p w c -> p (w c)"
+                    )
                 copy(
-                    out=x_sorted[:, :, part, lo:hi].rearrange("p u w g (c i) -> p (w g) c u i", i=4),
-                    in_=x_sb[:, part, first_col + lo : first_col + hi]
-                    .rearrange("p w c -> p (w c)")
-                    .bitcast(F32)
-                    .rearrange("p (k c i u) -> p k c u i", k=(hi - lo) * PASSES, i=4, u=2),
+                    out=x_sorted[:].rearrange("p u w g (c i) -> p (w g c) u i", i=4),
+                    in_=x_words.bitcast(F32).rearrange("p (c i u) -> p c u i", i=4, u=2),
                 )
+                for col in range(lo, hi):
+                    sorted_tiles[s, part, col] = x_sorted[:, :, col - lo]
 
             sort(nc.vector.tensor_copy, REAL, 0, cols)
             sort(nc.vector.tensor_copy, IMAG, 0, 1)
             if cols > 1:
                 sort(nc.scalar.copy, IMAG, 1, cols)
-            sorted_tiles[s] = x_sorted
 
         def transpose(s):
             cols = units[s][3]
-            x_sorted = sorted_tiles[s]
             grouped = mx_pool.tile([P, PARTS, cols, PASSES, P, PACK], BF16, align_bytes=64)
             grouped_words = (
                 grouped[:]
@@ -159,7 +168,7 @@ def tile_dot_pa_t_e_kernel(
                     for g in range(PASSES):
                         for u in range(2):
                             nc.tensor.transpose(
-                                turned[:, g, u, :], x_sorted[:, u, part, col, g, :], identity[:]
+                                turned[:, g, u, :], sorted_tiles[s, part, col][:, u, g, :], identity[:]
                             )
                     nc.scalar.copy(
                         out=grouped_words[:, part, col],
@@ -249,9 +258,9 @@ def tile_dot_pa_t_e_kernel(
                 load_x(tile_index)
 
         load_x(0)
-        load_x_column(0)
+        load_x_column(0, 0)
         load_scales(REAL, 0)
-        load_x_column(1)
+        load_x_column(0, 1)
         load_words(REAL, 0, 0, PASSES)
         load_words(IMAG, 0, 0, PASSES)
         load_scales(IMAG, 0)

@@ -52,10 +52,10 @@ def tile_dot_pa_t_e_kernel(
         def rows_of(batch_tile):
             return slice(batch_tile * P, (batch_tile + 1) * P)
 
-        identity = const.tile([P, P], F32)
+        identity = const.tile([P, P], F32, align_bytes=256)
         make_identity(nc, identity[:])
-        w_words = const.tile([P, PARTS, PIXEL_ROWS, ROW_GROUPS, FEATURES], U32, align_bytes=64)
-        w_planes = const.tile([P, PARTS, PIXEL_ROWS, FEATURES], U8, align_bytes=64)
+        w_words = const.tile([P, PARTS, PIXEL_ROWS, ROW_GROUPS, FEATURES], U32, align_bytes=256)
+        w_planes = const.tile([P, PARTS, PIXEL_ROWS, FEATURES], U8, align_bytes=256)
         nc.vector.memset(w_planes[:].rearrange("p a h n -> p (a h n)").bitcast(I32), 0)
 
         ones = const.tile([P, P], BF16)
@@ -64,7 +64,7 @@ def tile_dot_pa_t_e_kernel(
         nc.vector.memset(bias_rows[:], 0.0)
         nc.gpsimd.dma_start(out=bias_rows[0:1, REAL, :], in_=b_r.unsqueeze(0))
         nc.gpsimd.dma_start(out=bias_rows[0:1, IMAG, :], in_=b_i.unsqueeze(0))
-        bias = const.tile([P, PARTS, FEATURES], F32)
+        bias = const.tile([P, PARTS, FEATURES], F32, align_bytes=256)
 
         def spread_bias():
             bias_spread = sum_pool.tile([P, PARTS, FEATURES], F32, tag="sum")
@@ -89,9 +89,9 @@ def tile_dot_pa_t_e_kernel(
         def load_x(tile_index):
             pixel_row, batch_tile = divmod(tile_index, BATCH_TILES)
             if tile_index < HEAD_TILES:
-                x_sb = x_pool.tile([P, PIXEL_COLS, PARTS, CHANNELS], BF16)
+                x_sb = x_pool.tile([P, PIXEL_COLS, PARTS, CHANNELS], BF16, align_bytes=256)
             else:
-                x_sb = x_pool.tile([P, PARTS, PIXEL_COLS, CHANNELS], BF16)
+                x_sb = x_pool.tile([P, PARTS, PIXEL_COLS, CHANNELS], BF16, align_bytes=256)
             x_tiles[tile_index] = x_sb
             if tile_index >= HEAD_TILES:
                 for part in range(PARTS):
@@ -134,7 +134,9 @@ def tile_dot_pa_t_e_kernel(
             tile_index = pixel_row * BATCH_TILES + batch_tile
 
             def sort(copy, part, lo, hi):
-                x_sorted = mx_pool.tile([P, 2, hi - lo, PASSES, P], F32, tag="sorted%d%d" % (part, lo))
+                x_sorted = mx_pool.tile(
+                    [P, 2, hi - lo, PASSES, P], F32, tag="sorted%d%d" % (part, lo), align_bytes=256
+                )
                 if tile_index < HEAD_TILES:
                     x_words = x_tiles[tile_index][:, first_col, part]
                 else:
@@ -155,7 +157,7 @@ def tile_dot_pa_t_e_kernel(
 
         def transpose(s):
             cols = units[s][3]
-            grouped = mx_pool.tile([P, PARTS, cols, PASSES, P, PACK], BF16, align_bytes=64)
+            grouped = mx_pool.tile([P, PARTS, cols, PASSES, P, PACK], BF16, align_bytes=256)
             grouped_words = (
                 grouped[:]
                 .rearrange("p a w g b t -> p (a w g b t)")
@@ -178,8 +180,8 @@ def tile_dot_pa_t_e_kernel(
 
         def quantise(s, grouped):
             cols = units[s][3]
-            codes = mx_pool.tile([P, PARTS, cols, PASSES, P], U32, align_bytes=64)
-            planes = mx_pool.tile([P, PARTS, cols, PASSES, P], U8, align_bytes=64)
+            codes = mx_pool.tile([P, PARTS, cols, PASSES, P], U32, align_bytes=256)
+            planes = mx_pool.tile([P, PARTS, cols, PASSES, P], U8, align_bytes=256)
             for part in range(PARTS):
                 nc.vector.quantize_mx(
                     out=codes[:, part].rearrange("p w g b -> p (w g b)").bitcast(FP8X4),
@@ -221,8 +223,8 @@ def tile_dot_pa_t_e_kernel(
             cols = units[s][3]
             rr, im, ii = sums[s]
             shape = [P, cols, FEATURES]
-            rr_biased = out_pool.tile(shape, F32)
-            y = out_pool.tile([P, PARTS, cols, FEATURES], F32)
+            rr_biased = out_pool.tile(shape, F32, align_bytes=256)
+            y = out_pool.tile([P, PARTS, cols, FEATURES], F32, align_bytes=256)
             nc.vector.tensor_tensor(
                 out=rr_biased[:], in0=rr[:], in1=bias[:, REAL : REAL + 1, :].to_broadcast(shape), op=ALU.add
             )
@@ -234,7 +236,7 @@ def tile_dot_pa_t_e_kernel(
 
         def relu_and_store(s):
             pixel_row, batch_tile, first_col, cols = units[s]
-            result = result_pool.tile([P, PARTS, cols, FEATURES], F32)
+            result = result_pool.tile([P, PARTS, cols, FEATURES], F32, align_bytes=256)
             columns = slice(first_col, first_col + cols)
             if s < len(units) - 1:
                 nc.scalar.activation(out=result[:], in_=before_relu[s][:], func=RELU)

from contextlib import ExitStack

import concourse.mybir as mybir
from concourse.masks import make_identity

F32 = mybir.dt.float32
BF16 = mybir.dt.bfloat16
I32 = mybir.dt.int32
U32 = mybir.dt.uint32
U8 = mybir.dt.uint8
FP8X4 = mybir.dt.float8_e4m3fn_x4
ALU = mybir.AluOpType
RELU = mybir.ActivationFunctionType.Relu

P = 128
PACK = 4
BATCH, PARTS, PIXEL_ROWS, PIXEL_COLS, CHANNELS = 1024, 2, 2, 2, 1024
FEATURES = 256
REAL, IMAG = 0, 1
PASSES = CHANNELS // (P * PACK)
ROW_GROUPS = PIXEL_COLS * PASSES
BATCH_TILES = BATCH // P
ROUNDS = BATCH_TILES * PIXEL_ROWS
HEAD_TILES = 1
X_BUFS = 7

FLOPS = 2 * 4 * BATCH * PIXEL_ROWS * PIXEL_COLS * CHANNELS * FEATURES


def tile_dot_pa_t_e_kernel(
    tc, x_crop, W_r_words, W_r_scales, W_i_words, W_i_scales, b_r, b_i, out
):
    nc = tc.nc
    with ExitStack() as ctx:
        const = ctx.enter_context(tc.tile_pool(name="const", bufs=1))
        x_pool = ctx.enter_context(tc.tile_pool(name="x", bufs=X_BUFS))
        mx_pool = ctx.enter_context(tc.tile_pool(name="mx", bufs=2))
        out_pool = ctx.enter_context(tc.tile_pool(name="out", bufs=3))
        result_pool = ctx.enter_context(tc.tile_pool(name="result", bufs=8))
        turned_pool = ctx.enter_context(tc.psum_pool(name="turned", bufs=4))
        sum_pool = ctx.enter_context(tc.psum_pool(name="sums", bufs=4))
        ctx.enter_context(tc.manual_schedule())

        units = [(0, batch_tile, col, 1) for col in range(PIXEL_COLS) for batch_tile in range(HEAD_TILES)]
        for tile_index in range(ROUNDS):
            pixel_row, batch_tile = divmod(tile_index, BATCH_TILES)
            if tile_index == ROUNDS - 1:
                units.extend((pixel_row, batch_tile, col, 1) for col in range(PIXEL_COLS))
            elif tile_index >= HEAD_TILES:
                units.append((pixel_row, batch_tile, 0, PIXEL_COLS))

        def rows_of(batch_tile):
            return slice(batch_tile * P, (batch_tile + 1) * P)

        identity = const.tile([P, P], F32, align_bytes=256)
        make_identity(nc, identity[:])
        w_words = const.tile([P, PARTS, PIXEL_ROWS, ROW_GROUPS, FEATURES], U32, align_bytes=256)
        w_planes = const.tile([P, PARTS, PIXEL_ROWS, FEATURES], U8, align_bytes=256)
        nc.vector.memset(w_planes[:].rearrange("p a h n -> p (a h n)").bitcast(I32), 0)

        ones = const.tile([P, P], BF16)
        nc.vector.memset(ones[:], 1.0)
        bias_rows = const.tile([P, PARTS, FEATURES], BF16)
        nc.vector.memset(bias_rows[:], 0.0)
        nc.gpsimd.dma_start(out=bias_rows[0:1, REAL, :], in_=b_r.unsqueeze(0))
        nc.gpsimd.dma_start(out=bias_rows[0:1, IMAG, :], in_=b_i.unsqueeze(0))
        bias = const.tile([P, PARTS, FEATURES], F32, align_bytes=256)

        def spread_bias():
            bias_spread = sum_pool.tile([P, PARTS, FEATURES], F32, tag="sum")
            nc.tensor.matmul(
                out=bias_spread[:].rearrange("p a n -> p (a n)"),
                lhsT=ones[:],
                rhs=bias_rows[:].rearrange("p a n -> p (a n)"),
                start=True,
                stop=True,
            )
            nc.vector.tensor_copy(out=bias[:], in_=bias_spread[:])

        table_warmer = const.tile([P, 1], F32)
        nc.scalar.activation(out=table_warmer[:], in_=ones[:, 0:1], func=RELU)

        x_tiles = {}
        sorted_tiles = {}
        quantised = {}
        sums = {}
        before_relu = {}

        def load_x(tile_index):
            pixel_row, batch_tile = divmod(tile_index, BATCH_TILES)
            if tile_index < HEAD_TILES:
                x_sb = x_pool.tile([P, PIXEL_COLS, PARTS, CHANNELS], BF16, align_bytes=256)
            else:
                x_sb = x_pool.tile([P, PARTS, PIXEL_COLS, CHANNELS], BF16, align_bytes=256)
            x_tiles[tile_index] = x_sb
            if tile_index >= HEAD_TILES:
                for part in range(PARTS):
                    nc.sync.dma_start(
                        out=x_sb[:, part], in_=x_crop[rows_of(batch_tile), part, pixel_row, :, :]
                    )

        def load_x_column(batch_tile, col):
            nc.sync.dma_start(
                out=x_tiles[batch_tile][:, col], in_=x_crop[rows_of(batch_tile), :, 0, col, :]
            )

        def load_scales(part, pixel_row):
            groups = slice(pixel_row * ROW_GROUPS, (pixel_row + 1) * ROW_GROUPS)
            scales = (W_r_scales, W_i_scales)[part]
            for quadrant in range(4):
                nc.sync.dma_start(
                    out=w_planes[32 * quadrant : 32 * quadrant + 16, part, pixel_row, :].bitcast(I32),
                    in_=scales.bitcast(I32)[groups, 4 * quadrant : 4 * quadrant + 4, :],
                )

        def load_words(part, pixel_row, first_group=0, n_groups=ROW_GROUPS):
            row_groups = slice(first_group, first_group + n_groups)
            groups = slice(pixel_row * ROW_GROUPS + first_group, pixel_row * ROW_GROUPS + first_group + n_groups)
            words = (W_r_words, W_i_words)[part]
            as_words = words.rearrange("g p n t -> g p (n t)").bitcast(I32)
            nc.sync.dma_start(
                out=w_words[:, part, pixel_row, row_groups].bitcast(I32),
                in_=as_words[groups].rearrange("g p n -> p g n"),
            )

        def load_weights(pixel_row):
            for part in range(PARTS):
                load_scales(part, pixel_row)
            for part in range(PARTS):
                load_words(part, pixel_row)

        def sort_words(s):
            pixel_row, batch_tile, first_col, cols = units[s]
            tile_index = pixel_row * BATCH_TILES + batch_tile

            def sort(copy, part, lo, hi):
                x_sorted = mx_pool.tile(
                    [P, 2, hi - lo, PASSES, P], F32, tag="sorted%d%d" % (part, lo), align_bytes=256
                )
                if tile_index < HEAD_TILES:
                    x_words = x_tiles[tile_index][:, first_col, part]
                else:
                    x_words = x_tiles[tile_index][:, part, first_col + lo : first_col + hi].rearrange(
                        "p w c -> p (w c)"
                    )
                copy(
                    out=x_sorted[:].rearrange("p u w g (c i) -> p (w g c) u i", i=4),
                    in_=x_words.bitcast(F32).rearrange("p (c i u) -> p c u i", i=4, u=2),
                )
                for col in range(lo, hi):
                    sorted_tiles[s, part, col] = x_sorted[:, :, col - lo]

            sort(nc.vector.tensor_copy, REAL, 0, cols)
            sort(nc.vector.tensor_copy, IMAG, 0, 1)
            if cols > 1:
                sort(nc.scalar.copy, IMAG, 1, cols)

        def transpose(s):
            cols = units[s][3]
            grouped = mx_pool.tile([P, PARTS, cols, PASSES, P, PACK], BF16, align_bytes=256)
            grouped_words = (
                grouped[:]
                .rearrange("p a w g b t -> p (a w g b t)")
                .bitcast(F32)
                .rearrange("p (a w g b u) -> p a w g b u", a=PARTS, w=cols, g=PASSES, u=2)
            )
            for part in range(PARTS):
                for col in range(cols):
                    turned = turned_pool.tile([P, PASSES, 2, P], F32)
                    for g in range(PASSES):
                        for u in range(2):
                            nc.tensor.transpose(
                                turned[:, g, u, :], sorted_tiles[s, part, col][:, u, g, :], identity[:]
                            )
                    nc.scalar.copy(
                        out=grouped_words[:, part, col],
                        in_=turned[:].rearrange("p g u b -> p g b u"),
                    )
            return grouped

        def quantise(s, grouped):
            cols = units[s][3]
            codes = mx_pool.tile([P, PARTS, cols, PASSES, P], U32, align_bytes=256)
            planes = mx_pool.tile([P, PARTS, cols, PASSES, P], U8, align_bytes=256)
            for part in range(PARTS):
                nc.vector.quantize_mx(
                    out=codes[:, part].rearrange("p w g b -> p (w g b)").bitcast(FP8X4),
                    scales=planes[:, part].rearrange("p w g b -> p (w g b)"),
                    in_=grouped[:, part].rearrange("p w g b t -> p (w g b t)"),
                )
            quantised[s] = (codes, planes)

        def multiply(s):
            codes, planes = quantised[s]
            pixel_row, batch_tile, first_col, cols = units[s]
            rr = sum_pool.tile([P, cols, FEATURES], F32, tag="sum")
            im = sum_pool.tile([P, cols, FEATURES], F32, tag="sum")
            ii = sum_pool.tile([P, cols, FEATURES], F32, tag="sum")

            def group(acc, col, products):
                passes = [(x_part, w_part, g) for x_part, w_part in products for g in range(PASSES)]
                for n, (x_part, w_part, g) in enumerate(passes):
                    row_group = (first_col + col) * PASSES + g
                    nc.tensor.matmul_mx(
                        out=acc[:, col, :],
                        lhsT=codes[:, x_part, col, g, :].bitcast(FP8X4),
                        lhsT_scale=planes[:, x_part, col, g, :],
                        rhs=w_words[:, w_part, pixel_row, row_group, :].bitcast(FP8X4),
                        rhs_scale=w_planes[4 * row_group : P, w_part, pixel_row, :],
                        start=(n == 0),
                        stop=(n == len(passes) - 1),
                    )

            for col in range(cols):
                group(rr, col, [(REAL, REAL)])
            for col in range(cols):
                group(im, col, [(REAL, IMAG), (IMAG, REAL)])
            for col in range(cols):
                group(ii, col, [(IMAG, IMAG)])
            sums[s] = (rr, im, ii)

        def add_up(s):
            cols = units[s][3]
            rr, im, ii = sums[s]
            shape = [P, cols, FEATURES]
            rr_biased = out_pool.tile(shape, F32, align_bytes=256)
            y = out_pool.tile([P, PARTS, cols, FEATURES], F32, align_bytes=256)
            nc.vector.tensor_tensor(
                out=rr_biased[:], in0=rr[:], in1=bias[:, REAL : REAL + 1, :].to_broadcast(shape), op=ALU.add
            )
            nc.vector.tensor_tensor(
                out=y[:, IMAG], in0=im[:], in1=bias[:, IMAG : IMAG + 1, :].to_broadcast(shape), op=ALU.add
            )
            nc.vector.tensor_tensor(out=y[:, REAL], in0=rr_biased[:], in1=ii[:], op=ALU.subtract)
            before_relu[s] = y

        def relu_and_store(s):
            pixel_row, batch_tile, first_col, cols = units[s]
            result = result_pool.tile([P, PARTS, cols, FEATURES], F32, align_bytes=256)
            columns = slice(first_col, first_col + cols)
            if s < len(units) - 1:
                nc.scalar.activation(out=result[:], in_=before_relu[s][:], func=RELU)
                nc.sync.dma_start(out=out[rows_of(batch_tile), :, pixel_row, columns, :], in_=result[:])
            else:
                for part in (IMAG, REAL):
                    nc.scalar.activation(out=result[:, part], in_=before_relu[s][:, part], func=RELU)
                    nc.sync.dma_start(
                        out=out[rows_of(batch_tile), part, pixel_row, columns, :], in_=result[:, part]
                    )

        def refill(s):
            pixel_row, batch_tile, first_col, cols = units[s]
            if first_col + cols == PIXEL_COLS:
                load_next(pixel_row * BATCH_TILES + batch_tile + X_BUFS)

        def load_next(tile_index):
            if tile_index < ROUNDS:
                if tile_index % BATCH_TILES == 0:
                    load_weights(tile_index // BATCH_TILES)
                load_x(tile_index)

        load_x(0)
        load_x_column(0, 0)
        load_scales(REAL, 0)
        load_x_column(0, 1)
        load_words(REAL, 0, 0, PASSES)
        load_words(IMAG, 0, 0, PASSES)
        load_scales(IMAG, 0)
        load_x(1)
        load_words(REAL, 0, PASSES, PASSES)
        load_words(IMAG, 0, PASSES, PASSES)
        for tile_index in range(2, X_BUFS):
            load_next(tile_index)

        sort_words(0)
        refill(0)

        count = len(units)
        for step in range(count + 2):
            if step < count:
                grouped = transpose(step)
            if step >= 2:
                add_up(step - 2)
            if step + 1 < count:
                sort_words(step + 1)
                refill(step + 1)
            if step < count:
                quantise(step, grouped)
            if step == 1:
                spread_bias()
            if 1 <= step <= count:
                multiply(step - 1)
            if step >= 2:
                relu_and_store(step - 2)
